import numpy as np
import ml_dtypes


def mxq(x, axis, fmt="e4m3"):
    dtype, down = {"e4m3": (ml_dtypes.float8_e4m3fn, 7), "e5m2": (ml_dtypes.float8_e5m2, 14)}[fmt]
    v = np.moveaxis(np.asarray(x, np.float32).astype(ml_dtypes.bfloat16).astype(np.float64), axis, -1)
    blocks = v.reshape(v.shape[:-1] + (-1, 32))
    amax = np.abs(blocks).max(-1, keepdims=True)
    byte = np.maximum(np.where(amax > 0, np.frexp(amax)[1] - 1 + 127, 0) - down, 1)
    scale = np.exp2(byte - 127.0)
    codes = (blocks / scale).astype(np.float32).astype(dtype).astype(np.float64)
    return np.moveaxis((codes * scale).reshape(v.shape), -1, axis)


WIDE = False


def mx_kscale(k):
    if not WIDE:
        return np.ones(k)
    levels = np.array([10, -10, 5, -5, 0])
    if k % 512:
        return np.exp2(np.random.permutation(np.resize(levels, k // 32))).repeat(32)
    a = np.empty((k // 512, 16))
    for p in range(k // 512):
        a[p, :8] = np.random.permutation(np.resize(levels, 8))
        for g in range(8):
            far = levels[np.abs(levels - a[p, g]) >= 10]
            a[p, g + 8] = far[np.random.randint(len(far))]
    return np.exp2(a.ravel()).repeat(32)


BF16 = ml_dtypes.bfloat16


def bf(x):
    return np.asarray(x, np.float32).astype(BF16)


def f64(x):
    return np.asarray(x).astype(np.float64)


HI, WS, D, F, NH = 32, 4, 512, 2048, 8
EPS = 1e-5
N = HI * HI
NWS = HI // WS
NW = NWS * NWS
NPW = WS * WS
HD = D // NH
SH = WS // 2


def layer_norm(x, g, b):
    m = x.mean(-1, keepdims=True)
    v = ((x - m) ** 2).mean(-1, keepdims=True)
    return (x - m) / np.sqrt(v + EPS) * g + b


def win_part(img):
    return img.reshape(NWS, WS, NWS, WS, D).swapaxes(1, 2).reshape(NW, NPW, D)


def win_merge(win):
    return win.reshape(NWS, NWS, WS, WS, D).swapaxes(1, 2).reshape(HI, HI, D)


def heads(t):
    return np.ascontiguousarray(t.reshape(NW, NPW, NH, HD).swapaxes(1, 2))


def setup_inputs():
    s = mx_kscale(D)
    return {"x_win": bf(np.random.standard_normal((N, D)) * 1.5),
            "ln3_g": bf((1.0 + 0.1 * np.random.standard_normal(D)) * s),
            "ln3_b": bf(0.1 * np.random.standard_normal(D) * s),
            "qkv2_w": bf(np.random.standard_normal((D, 3 * D)) / np.sqrt(D) / s[:, None]),
            "qkv2_b": bf(0.1 * np.random.standard_normal(3 * D))}


def reference(x_win, ln3_g, ln3_b, qkv2_w, qkv2_b):
    h = layer_norm(f64(x_win), f64(ln3_g), f64(ln3_b))
    img = win_merge(h.reshape(NW, NPW, D))
    shifted = win_part(np.roll(img, (-SH, -SH), (0, 1))).reshape(N, D)
    qkv = (mxq(shifted, 1, "e4m3") @ mxq(f64(qkv2_w), 0, "e4m3")) + f64(qkv2_b)
    q, k, v = np.split(qkv, 3, axis=-1)
    return heads(q), heads(k), heads(v)

@@ -1,0 +1,270 @@
+from contextlib import ExitStack
+
+import concourse.mybir as mybir
+from concourse.masks import make_identity
+
+F32 = mybir.dt.float32
+BF16 = mybir.dt.bfloat16
+U32 = mybir.dt.uint32
+U8 = mybir.dt.uint8
+FP8X4 = mybir.dt.float8_e4m3fn_x4
+ACT = mybir.ActivationFunctionType
+ALU = mybir.AluOpType
+
+P = 128
+PACK = 4
+D = P * PACK
+GRID = 8
+WINDOWS = GRID * GRID
+LANES = 8
+ROW_LANES = 4
+ROUNDS = LANES // ROW_LANES
+PARTS = 3
+HEADS = 8
+HEAD_DIM = D // HEADS
+PASS_HEADS = 4
+PASS_COLS = PASS_HEADS * HEAD_DIM
+BANK_LANES = 2
+LOAD_LANES = 2
+EPS = 1e-5
+
+FLOPS = 2 * (P * LANES) * D * (PARTS * D)
+
+
+def tile_swintransformerblock_pa_kernel(
+    tc, x_win, ln3_g, ln3_b, qkv2_w, qkv2_b, out_0, out_1, out_2
+):
+    nc = tc.nc
+    outs = (out_0, out_1, out_2)
+
+    with ExitStack() as ctx:
+        ctx.enter_context(tc.manual_schedule())
+        const = ctx.enter_context(tc.tile_pool(name="const", bufs=1))
+        keep = ctx.enter_context(tc.tile_pool(name="keep", bufs=1))
+        small = ctx.enter_context(tc.tile_pool(name="small", bufs=2))
+        z_pool = ctx.enter_context(tc.tile_pool(name="z_pool", bufs=4))
+        stage = ctx.enter_context(tc.tile_pool(name="stage", bufs=3))
+        t_psum = ctx.enter_context(tc.psum_pool(name="t_psum", bufs=1))
+        acc_psum = ctx.enter_context(tc.psum_pool(name="acc_psum", bufs=4))
+
+        x_sb = keep.tile([P, LANES, D], BF16)
+        x_rows = x_win.rearrange("(i j) d -> i j d", j=LANES)
+        w_sb = keep.tile([P, PARTS, PACK, D], BF16)
+        w_rows = qkv2_w.rearrange("(p t) (s n) -> p s t n", p=P, s=PARTS)
+        gain_raw = const.tile([P, PACK], BF16)
+        bias_raw = const.tile([P, PACK], BF16)
+        bias_all = const.tile([P, PARTS, D], BF16)
+
+        def load_x(lane0):
+            lanes = slice(lane0, lane0 + LOAD_LANES)
+            nc.sync.dma_start(out=x_sb[:, lanes, :], in_=x_rows[:, lanes, :])
+
+        def load_w(s):
+            nc.sync.dma_start(out=w_sb[:, s, :, :], in_=w_rows[:, s, :, :])
+
+        load_x(0)
+        load_x(LOAD_LANES)
+        nc.sync.dma_start(out=gain_raw[:], in_=ln3_g.rearrange("(p t) -> p t", p=P))
+        nc.sync.dma_start(out=bias_raw[:], in_=ln3_b.rearrange("(p t) -> p t", p=P))
+        load_w(0)
+        load_x(2 * LOAD_LANES)
+        load_x(3 * LOAD_LANES)
+        load_w(1)
+        load_w(2)
+        nc.sync.dma_start(
+            out=bias_all[:].rearrange("m s n -> m (s n)"), in_=qkv2_b.partition_broadcast(P)
+        )
+
+        eps = const.tile([P, 1], F32)
+        nc.vector.memset(eps[:], EPS)
+        table_warmer = const.tile([P, 1], F32)
+        nc.scalar.activation(out=table_warmer[:], in_=eps[:], func=ACT.Sqrt)
+
+        ident = const.tile([P, P], F32)
+        make_identity(nc, ident[:])
+
+        take_below = const.tile([P, P], F32)
+        from_half = ident[:].rearrange("i (w h) -> i w h", h=2)
+        to_half = take_below[:].rearrange("i (w h) -> i w h", h=2)
+        nc.vector.tensor_copy(out=to_half[:, :, 0], in_=from_half[:, :, 1])
+        nc.vector.tensor_copy(
+            out=to_half[:, 0 : WINDOWS - GRID, 1], in_=from_half[:, GRID:WINDOWS, 0]
+        )
+        nc.vector.tensor_copy(
+            out=to_half[:, WINDOWS - GRID : WINDOWS, 1], in_=from_half[:, 0:GRID, 0]
+        )
+        take_below_right = const.tile([P, P], F32)
+        from_row = take_below[:].rearrange("i (r e) -> i r e", e=2 * GRID)
+        to_row = take_below_right[:].rearrange("i (r e) -> i r e", e=2 * GRID)
+        nc.vector.tensor_copy(out=to_row[:, :, 0 : 2 * GRID - 2], in_=from_row[:, :, 2 : 2 * GRID])
+        nc.vector.tensor_copy(out=to_row[:, :, 2 * GRID - 2 : 2 * GRID], in_=from_row[:, :, 0:2])
+
+        s_codes = keep.tile([P, ROUNDS, ROW_LANES * P], U32, align_bytes=64)
+        s_scales = keep.tile([P, ROUNDS, ROW_LANES * P], U8, align_bytes=64)
+        w_codes = keep.tile([P, PARTS, D], U32, align_bytes=64)
+        w_scales = keep.tile([P, PARTS, D], U8, align_bytes=64)
+        out_sb = keep.tile([P, PARTS, HEADS, LANES, HEAD_DIM], F32)
+
+        gain_cols = const.tile([P, 2 * PACK], F32)
+
+        def regroup(copy, planes, name):
+            grouped = stage.tile([P, D, PACK], BF16, align_bytes=64, name=name, tag=name)
+            copy(
+                out=grouped[:].rearrange("p (c i) t -> p c t i", i=4),
+                in_=planes.rearrange("p t (c i) -> p c t i", i=4),
+            )
+            return grouped
+
+        def quantise(grouped, codes, scales):
+            nc.vector.quantize_mx(
+                out=codes.bitcast(FP8X4),
+                scales=scales,
+                in_=grouped[:].rearrange("p c t -> p (c t)"),
+            )
+
+        def row_moments(r):
+            stats = small.tile([P, ROW_LANES, 6], F32)
+            mean_var = small.tile([P, ROW_LANES, 2], F32)
+            for u in range(ROW_LANES):
+                nc.vector.bn_stats(out=stats[:, u, :], in_=x_sb[:, r * ROW_LANES + u, :])
+            for u in range(ROW_LANES):
+                nc.vector.bn_aggr(out=mean_var[:, u, :], in_=stats[:, u, :])
+            return mean_var
+
+        def row_scales(mean_var):
+            std = small.tile([P, ROW_LANES], F32)
+            nc.scalar.activation(out=std[:], in_=mean_var[:, :, 1], func=ACT.Sqrt, bias=eps[:])
+            rstd = small.tile([P, ROW_LANES], F32)
+            nc.vector.reciprocal(out=rstd[:], in_=std[:])
+            shift = small.tile([P, ROW_LANES], F32)
+            nc.vector.scalar_tensor_tensor(
+                out=shift[:],
+                in0=mean_var[:, :, 0],
+                scalar=-1.0,
+                in1=rstd[:],
+                op0=ALU.mult,
+                op1=ALU.mult,
+            )
+            return rstd, shift
+
+        def normalise_and_transpose(r, rstd, shift):
+            z_banks = [
+                t_psum.tile([P, ROW_LANES, P], F32, name="z_bank%d" % t, tag="z_bank%d" % t)
+                for t in range(PACK)
+            ]
+            for u in range(ROW_LANES):
+                z = z_pool.tile([P, D], F32)
+                z_out = z[:].rearrange("i (t p) -> i t p", t=PACK)
+                x_in = x_sb[:, r * ROW_LANES + u, :].rearrange("i (p t) -> i t p", t=PACK)
+                if u < ROW_LANES // 2:
+                    nc.scalar.activation(
+                        out=z_out,
+                        in_=x_in,
+                        func=ACT.Identity,
+                        scale=rstd[:, u : u + 1],
+                        bias=shift[:, u : u + 1],
+                    )
+                else:
+                    nc.gpsimd.tensor_scalar(
+                        out=z_out,
+                        in0=x_in,
+                        scalar1=rstd[:, u : u + 1],
+                        scalar2=shift[:, u : u + 1],
+                        op0=ALU.mult,
+                        op1=ALU.add,
+                    )
+                q = (u + 2) % ROW_LANES
+                permutation = take_below_right if u < 2 else take_below
+                for t in range(PACK):
+                    nc.tensor.transpose(
+                        out=z_banks[t][:, q, :],
+                        in_=z[:, t * P : (t + 1) * P],
+                        identity=permutation[:],
+                    )
+            return z_banks
+
+        def gain_out_of_psum(z_banks, vector_banks):
+            h_planes = stage.tile([P, PACK, ROW_LANES * P], BF16)
+            for t in range(PACK):
+                z_bank = z_banks[t][:].rearrange("p q m -> p (q m)")
+                gain = gain_cols[:, t : t + 1]
+                bias = gain_cols[:, PACK + t : PACK + t + 1]
+                if t < PACK - vector_banks:
+                    nc.scalar.activation(
+                        out=h_planes[:, t, :], in_=z_bank, func=ACT.Identity, scale=gain, bias=bias
+                    )
+                else:
+                    nc.vector.tensor_scalar(
+                        out=h_planes[:, t, :],
+                        in0=z_bank,
+                        scalar1=gain,
+                        scalar2=bias,
+                        op0=ALU.mult,
+                        op1=ALU.add,
+                    )
+            return h_planes
+
+        def project(r, s):
+            dram = outs[s].rearrange("w n (h r q) c -> h r w n (q c)", h=2, r=ROUNDS)
+            for n0 in range(0, HEADS, PASS_HEADS):
+                cols = slice(n0 * HEAD_DIM, n0 * HEAD_DIM + PASS_COLS)
+                for q0 in range(0, ROW_LANES, BANK_LANES):
+                    acc = acc_psum.tile([P, BANK_LANES, PASS_COLS], F32, tag="acc")
+                    for e in range(BANK_LANES):
+                        rows = slice((q0 + e) * P, (q0 + e + 1) * P)
+                        nc.tensor.matmul_mx(
+                            out=acc[:, e, :],
+                            lhsT=s_codes[:, r, rows].bitcast(FP8X4),
+                            lhsT_scale=s_scales[:, r, rows],
+                            rhs=w_codes[:, s, cols].bitcast(FP8X4),
+                            rhs_scale=w_scales[:, s, cols],
+                            start=True,
+                            stop=True,
+                        )
+                    lane0 = r * ROW_LANES + q0
+                    nc.vector.tensor_tensor(
+                        out=out_sb[
+                            :, s, n0 : n0 + PASS_HEADS, lane0 : lane0 + BANK_LANES, :
+                        ].rearrange("m n q c -> m q n c"),
+                        in0=acc[:].rearrange("m q (n c) -> m q n c", c=HEAD_DIM),
+                        in1=bias_all[:, s, cols]
+                        .rearrange("m (o n c) -> m o n c", o=1, c=HEAD_DIM)
+                        .to_broadcast([P, BANK_LANES, PASS_HEADS, HEAD_DIM]),
+                        op=ALU.add,
+                    )
+                for half in range(2):
+                    nc.sync.dma_start(
+                        out=dram[half, r, :, n0 : n0 + PASS_HEADS, :],
+                        in_=out_sb[
+                            half:P:2,
+                            s,
+                            n0 : n0 + PASS_HEADS,
+                            r * ROW_LANES : (r + 1) * ROW_LANES,
+                            :,
+                        ].rearrange("m n q c -> m n (q c)"),
+                    )
+
+        mean_var0 = row_moments(0)
+        nc.vector.tensor_copy(out=gain_cols[:, 0:PACK], in_=gain_raw[:])
+        nc.vector.tensor_copy(out=gain_cols[:, PACK : 2 * PACK], in_=bias_raw[:])
+        rstd0, shift0 = row_scales(mean_var0)
+        z_banks0 = normalise_and_transpose(0, rstd0, shift0)
+        rstd1, shift1 = row_scales(row_moments(1))
+        h_planes0 = gain_out_of_psum(z_banks0, vector_banks=2)
+        z_banks1 = normalise_and_transpose(1, rstd1, shift1)
+        w_grouped0 = regroup(nc.vector.tensor_copy, w_sb[:, 0, :, :], "w_grouped")
+        h_grouped0 = regroup(nc.vector.tensor_copy, h_planes0[:], "h_grouped")
+        quantise(w_grouped0, w_codes[:, 0, :], w_scales[:, 0, :])
+        w_grouped1 = regroup(nc.scalar.copy, w_sb[:, 1, :, :], "w_grouped")
+        quantise(h_grouped0, s_codes[:, 0, :], s_scales[:, 0, :])
+        quantise(w_grouped1, w_codes[:, 1, :], w_scales[:, 1, :])
+        w_grouped2 = regroup(nc.scalar.copy, w_sb[:, 2, :, :], "w_grouped")
+        h_planes1 = gain_out_of_psum(z_banks1, vector_banks=0)
+        h_grouped1 = regroup(nc.scalar.copy, h_planes1[:], "h_grouped")
+        project(0, 0)
+        quantise(w_grouped2, w_codes[:, 2, :], w_scales[:, 2, :])
+        project(0, 1)
+        quantise(h_grouped1, s_codes[:, 1, :], s_scales[:, 1, :])
+        project(0, 2)
+        for s in range(PARTS):
+            project(1, s)

@@ -26,6 +26,7 @@ PASS_HEADS = 4
 PASS_COLS = PASS_HEADS * HEAD_DIM
 BANK_LANES = 2
 LOAD_LANES = 2
+PAIR = 2
 EPS = 1e-5
 
 FLOPS = 2 * (P * LANES) * D * (PARTS * D)
@@ -41,10 +42,10 @@ def tile_swintransformerblock_pa_kernel(
         ctx.enter_context(tc.manual_schedule())
         const = ctx.enter_context(tc.tile_pool(name="const", bufs=1))
         keep = ctx.enter_context(tc.tile_pool(name="keep", bufs=1))
-        small = ctx.enter_context(tc.tile_pool(name="small", bufs=2))
+        small = ctx.enter_context(tc.tile_pool(name="small", bufs=1))
         z_pool = ctx.enter_context(tc.tile_pool(name="z_pool", bufs=4))
-        stage = ctx.enter_context(tc.tile_pool(name="stage", bufs=3))
-        t_psum = ctx.enter_context(tc.psum_pool(name="t_psum", bufs=1))
+        stage = ctx.enter_context(tc.tile_pool(name="stage", bufs=1))
+        z_psum = ctx.enter_context(tc.psum_pool(name="z_psum", bufs=2))
         acc_psum = ctx.enter_context(tc.psum_pool(name="acc_psum", bufs=4))
 
         x_sb = keep.tile([P, LANES, D], BF16)
@@ -55,25 +56,26 @@ def tile_swintransformerblock_pa_kernel(
         bias_raw = const.tile([P, PACK], BF16)
         bias_all = const.tile([P, PARTS, D], BF16)
 
-        def load_x(lane0):
-            lanes = slice(lane0, lane0 + LOAD_LANES)
+        def load_x(lane0, lanes=LOAD_LANES):
+            lanes = slice(lane0, lane0 + lanes)
             nc.sync.dma_start(out=x_sb[:, lanes, :], in_=x_rows[:, lanes, :])
 
         def load_w(s):
             nc.sync.dma_start(out=w_sb[:, s, :, :], in_=w_rows[:, s, :, :])
 
-        load_x(0)
+        load_x(0, 1)
+        load_x(1, 1)
         load_x(LOAD_LANES)
+        load_w(0)
         nc.sync.dma_start(out=gain_raw[:], in_=ln3_g.rearrange("(p t) -> p t", p=P))
         nc.sync.dma_start(out=bias_raw[:], in_=ln3_b.rearrange("(p t) -> p t", p=P))
-        load_w(0)
         load_x(2 * LOAD_LANES)
         load_x(3 * LOAD_LANES)
         load_w(1)
-        load_w(2)
         nc.sync.dma_start(
             out=bias_all[:].rearrange("m s n -> m (s n)"), in_=qkv2_b.partition_broadcast(P)
         )
+        load_w(2)
 
         eps = const.tile([P, 1], F32)
         nc.vector.memset(eps[:], EPS)
@@ -107,164 +109,382 @@ def tile_swintransformerblock_pa_kernel(
 
         gain_cols = const.tile([P, 2 * PACK], F32)
 
-        def regroup(copy, planes, name):
-            grouped = stage.tile([P, D, PACK], BF16, align_bytes=64, name=name, tag=name)
+        def regroup(engine, planes, grouped):
+            if engine is nc.gpsimd:
+                nc.gpsimd.tensor_scalar(
+                    out=grouped,
+                    in0=planes.rearrange("p t c -> p c t"),
+                    scalar1=1.0,
+                    scalar2=0.0,
+                    op0=ALU.mult,
+                    op1=ALU.add,
+                )
+                return
+            copy = nc.scalar.copy if engine is nc.scalar else nc.vector.tensor_copy
             copy(
-                out=grouped[:].rearrange("p (c i) t -> p c t i", i=4),
+                out=grouped.rearrange("p (c i) t -> p c t i", i=4),
                 in_=planes.rearrange("p t (c i) -> p c t i", i=4),
             )
-            return grouped
 
         def quantise(grouped, codes, scales):
             nc.vector.quantize_mx(
                 out=codes.bitcast(FP8X4),
                 scales=scales,
-                in_=grouped[:].rearrange("p c t -> p (c t)"),
+                in_=grouped.rearrange("p c t -> p (c t)"),
             )
 
-        def row_moments(r):
-            stats = small.tile([P, ROW_LANES, 6], F32)
-            mean_var = small.tile([P, ROW_LANES, 2], F32)
-            for u in range(ROW_LANES):
-                nc.vector.bn_stats(out=stats[:, u, :], in_=x_sb[:, r * ROW_LANES + u, :])
-            for u in range(ROW_LANES):
-                nc.vector.bn_aggr(out=mean_var[:, u, :], in_=stats[:, u, :])
-            return mean_var
+        stats = keep.tile([P, LANES, 6], F32)
+        mean_var = keep.tile([P, LANES, 2], F32)
+        std = [small.tile([P, PAIR], F32, name="std%d" % j) for j in range(LANES // PAIR)]
+        rstd = [small.tile([P, PAIR], F32, name="rstd%d" % j) for j in range(LANES // PAIR)]
+        shift = [small.tile([P, PAIR], F32, name="shift%d" % j) for j in range(LANES // PAIR)]
 
-        def row_scales(mean_var):
-            std = small.tile([P, ROW_LANES], F32)
-            nc.scalar.activation(out=std[:], in_=mean_var[:, :, 1], func=ACT.Sqrt, bias=eps[:])
-            rstd = small.tile([P, ROW_LANES], F32)
-            nc.vector.reciprocal(out=rstd[:], in_=std[:])
-            shift = small.tile([P, ROW_LANES], F32)
+        def row_stats(lane):
+            nc.vector.bn_stats(out=stats[:, lane, :], in_=x_sb[:, lane, :])
+
+        def row_moments(j):
+            for lane in range(PAIR * j, PAIR * j + PAIR):
+                nc.vector.bn_aggr(out=mean_var[:, lane, :], in_=stats[:, lane, :])
+
+        neg_mean = [small.tile([P, 1], F32, name="neg_mean%d" % j) for j in range(LANES)]
+        dev_sum = [small.tile([P, 1], F32, name="dev_sum%d" % j) for j in range(LANES)]
+        dump = keep.tile([P, D], BF16)
+
+        def neg_mean_on_scalar(lane):
+            nc.scalar.activation(
+                out=dump[:],
+                in_=x_sb[:, lane, :],
+                func=ACT.Identity,
+                scale=-1.0 / D,
+                accum_out=neg_mean[lane][:],
+            )
+
+        def dev_sum_on_scalar(lane):
+            nc.scalar.activation(
+                out=dump[:],
+                in_=x_sb[:, lane, :],
+                func=ACT.Square,
+                bias=neg_mean[lane][:],
+                accum_out=dev_sum[lane][:],
+            )
+
+        def lane_std(lane, from_scalar):
+            j, e = divmod(lane, PAIR)
+            nc.scalar.activation(
+                out=std[j][:, e : e + 1],
+                in_=dev_sum[lane][:] if from_scalar else mean_var[:, lane, 1:2],
+                func=ACT.Sqrt,
+                bias=eps[:],
+                scale=1.0 / D if from_scalar else 1.0,
+            )
+
+        def lane_moments(lane):
+            nc.vector.bn_aggr(out=mean_var[:, lane, :], in_=stats[:, lane, :])
+
+        def row_std(j):
+            nc.scalar.activation(
+                out=std[j][:],
+                in_=mean_var[:, PAIR * j : PAIR * j + PAIR, 1],
+                func=ACT.Sqrt,
+                bias=eps[:],
+            )
+
+        def row_scales(j, with_shift):
+            nc.vector.reciprocal(out=rstd[j][:], in_=std[j][:])
+            if with_shift:
+                nc.vector.scalar_tensor_tensor(
+                    out=shift[j][:],
+                    in0=mean_var[:, PAIR * j : PAIR * j + PAIR, 0],
+                    scalar=-1.0,
+                    in1=rstd[j][:],
+                    op0=ALU.mult,
+                    op1=ALU.mult,
+                )
+
+        def lane_rstd(lane):
+            j, e = divmod(lane, PAIR)
+            nc.vector.reciprocal(out=rstd[j][:, e : e + 1], in_=std[j][:, e : e + 1])
+
+        def lane_shift(lane, from_scalar=False):
+            j, e = divmod(lane, PAIR)
             nc.vector.scalar_tensor_tensor(
-                out=shift[:],
-                in0=mean_var[:, :, 0],
-                scalar=-1.0,
-                in1=rstd[:],
+                out=shift[j][:, e : e + 1],
+                in0=neg_mean[lane][:] if from_scalar else mean_var[:, lane, 0:1],
+                scalar=1.0 if from_scalar else -1.0,
+                in1=rstd[j][:, e : e + 1],
                 op0=ALU.mult,
                 op1=ALU.mult,
             )
-            return rstd, shift
 
-        def normalise_and_transpose(r, rstd, shift):
-            z_banks = [
-                t_psum.tile([P, ROW_LANES, P], F32, name="z_bank%d" % t, tag="z_bank%d" % t)
-                for t in range(PACK)
+        def normalise(lane, engine, from_scalar=False):
+            z = z_pool.tile([P, D], F32)
+            z_out = z[:].rearrange("i (t p) -> i t p", t=PACK)
+            x_in = x_sb[:, lane, :].rearrange("i (p t) -> i t p", t=PACK)
+            j, e = divmod(lane, PAIR)
+            if engine is nc.scalar:
+                nc.scalar.activation(
+                    out=z_out,
+                    in_=x_in,
+                    func=ACT.Identity,
+                    scale=rstd[j][:, e : e + 1],
+                    bias=shift[j][:, e : e + 1],
+                )
+            elif engine is nc.vector:
+                nc.vector.tensor_scalar(
+                    out=z_out,
+                    in0=x_in,
+                    scalar1=neg_mean[lane][:] if from_scalar else mean_var[:, lane, 0:1],
+                    scalar2=rstd[j][:, e : e + 1],
+                    op0=ALU.add if from_scalar else ALU.subtract,
+                    op1=ALU.mult,
+                )
+            else:
+                nc.gpsimd.tensor_scalar(
+                    out=z_out,
+                    in0=x_in,
+                    scalar1=rstd[j][:, e : e + 1],
+                    scalar2=shift[j][:, e : e + 1],
+                    op0=ALU.mult,
+                    op1=ALU.add,
+                )
+            return z
+
+        def new_z_banks():
+            return [
+                z_psum.tile([P, 2, PAIR * P], F32, name="z_bank%d" % b, tag="z_bank%d" % b)
+                for b in range(2)
             ]
-            for u in range(ROW_LANES):
-                z = z_pool.tile([P, D], F32)
-                z_out = z[:].rearrange("i (t p) -> i t p", t=PACK)
-                x_in = x_sb[:, r * ROW_LANES + u, :].rearrange("i (p t) -> i t p", t=PACK)
-                if u < ROW_LANES // 2:
-                    nc.scalar.activation(
-                        out=z_out,
-                        in_=x_in,
-                        func=ACT.Identity,
-                        scale=rstd[:, u : u + 1],
-                        bias=shift[:, u : u + 1],
-                    )
-                else:
-                    nc.gpsimd.tensor_scalar(
-                        out=z_out,
-                        in0=x_in,
-                        scalar1=rstd[:, u : u + 1],
-                        scalar2=shift[:, u : u + 1],
-                        op0=ALU.mult,
-                        op1=ALU.add,
-                    )
-                q = (u + 2) % ROW_LANES
-                permutation = take_below_right if u < 2 else take_below
-                for t in range(PACK):
-                    nc.tensor.transpose(
-                        out=z_banks[t][:, q, :],
-                        in_=z[:, t * P : (t + 1) * P],
-                        identity=permutation[:],
-                    )
-            return z_banks
 
-        def gain_out_of_psum(z_banks, vector_banks):
-            h_planes = stage.tile([P, PACK, ROW_LANES * P], BF16)
+        def transpose(lane, z, z_banks):
+            u = lane % ROW_LANES
+            permutation = take_below_right if u < 2 else take_below
+            e = lane % PAIR
             for t in range(PACK):
-                z_bank = z_banks[t][:].rearrange("p q m -> p (q m)")
-                gain = gain_cols[:, t : t + 1]
-                bias = gain_cols[:, PACK + t : PACK + t + 1]
-                if t < PACK - vector_banks:
-                    nc.scalar.activation(
-                        out=h_planes[:, t, :], in_=z_bank, func=ACT.Identity, scale=gain, bias=bias
-                    )
-                else:
-                    nc.vector.tensor_scalar(
-                        out=h_planes[:, t, :],
-                        in0=z_bank,
-                        scalar1=gain,
-                        scalar2=bias,
-                        op0=ALU.mult,
-                        op1=ALU.add,
-                    )
-            return h_planes
+                nc.tensor.transpose(
+                    out=z_banks[t // 2][:, t % 2, e * P : (e + 1) * P],
+                    in_=z[:, t * P : (t + 1) * P],
+                    identity=permutation[:],
+                )
 
-        def project(r, s):
+        h_planes = [stage.tile([P, PACK, PAIR * P], BF16, name="h_planes%d" % j) for j in range(4)]
+        h_grouped = [
+            stage.tile([P, PAIR * P, PACK], BF16, align_bytes=64, name="h_grouped%d" % j)
+            for j in range(4)
+        ]
+
+        def gain_out_of_psum(j, z_banks, t, engine):
+            z_bank = z_banks[t // 2][:, t % 2, :]
+            gain = gain_cols[:, t : t + 1]
+            bias = gain_cols[:, PACK + t : PACK + t + 1]
+            if engine is nc.scalar:
+                nc.scalar.activation(
+                    out=h_planes[j][:, t, :], in_=z_bank, func=ACT.Identity, scale=gain, bias=bias
+                )
+            else:
+                nc.vector.tensor_scalar(
+                    out=h_planes[j][:, t, :],
+                    in0=z_bank,
+                    scalar1=gain,
+                    scalar2=bias,
+                    op0=ALU.mult,
+                    op1=ALU.add,
+                )
+
+        def pair_cols(j):
+            q0 = (PAIR * j + 2) % ROW_LANES
+            return j // 2, slice(q0 * P, (q0 + PAIR) * P)
+
+        def quantise_h(j):
+            r, rows = pair_cols(j)
+            quantise(h_grouped[j][:], s_codes[:, r, rows], s_scales[:, r, rows])
+
+        w_grouped = [
+            stage.tile([P, D, PACK], BF16, align_bytes=64, name="w_grouped%d" % s)
+            for s in range(PARTS)
+        ]
+        lo = slice(0, PASS_COLS)
+        hi = slice(PASS_COLS, D)
+        full = slice(0, D)
+
+        def regroup_w(engine, s, cols):
+            regroup(engine, w_sb[:, s, :, cols], w_grouped[s][:, cols, :])
+
+        def quantise_w(s, cols):
+            quantise(w_grouped[s][:, cols, :], w_codes[:, s, cols], w_scales[:, s, cols])
+
+        def group_out(s, n0, lane0):
+            return out_sb[
+                :, s, n0 : n0 + PASS_HEADS, lane0 : lane0 + BANK_LANES, :
+            ].rearrange("m n q c -> m q n c")
+
+        def bias_of(s, n0):
+            return (
+                bias_all[:, s, n0 * HEAD_DIM : n0 * HEAD_DIM + PASS_COLS]
+                .rearrange("m (o n c) -> m o n c", o=1, c=HEAD_DIM)
+                .to_broadcast([P, BANK_LANES, PASS_HEADS, HEAD_DIM])
+            )
+
+        def multiply(j, s, n0, pool, tag):
+            r, rows0 = pair_cols(j)
+            cols = slice(n0 * HEAD_DIM, n0 * HEAD_DIM + PASS_COLS)
+            acc = pool.tile([P, BANK_LANES, PASS_COLS], F32, name="acc", tag=tag)
+            for e in range(BANK_LANES):
+                rows = slice(rows0.start + e * P, rows0.start + (e + 1) * P)
+                nc.tensor.matmul_mx(
+                    out=acc[:, e, :],
+                    lhsT=s_codes[:, r, rows].bitcast(FP8X4),
+                    lhsT_scale=s_scales[:, r, rows],
+                    rhs=w_codes[:, s, cols].bitcast(FP8X4),
+                    rhs_scale=w_scales[:, s, cols],
+                    start=True,
+                    stop=True,
+                )
+            return acc
+
+        def out_of_bank(j, s, n0):
+            r, rows0 = pair_cols(j)
+            return group_out(s, n0, r * ROW_LANES + rows0.start // P)
+
+        def vec(j, s, n0):
+            acc = multiply(j, s, n0, acc_psum, "acc")
+            nc.vector.tensor_tensor(
+                out=out_of_bank(j, s, n0),
+                in0=acc[:].rearrange("m q (n c) -> m q n c", c=HEAD_DIM),
+                in1=bias_of(s, n0),
+                op=ALU.add,
+            )
+
+        def side(j, s, n0):
+            acc = multiply(j, s, n0, z_psum, "z_bank%d" % (j % 2))
+            out = out_of_bank(j, s, n0)
+            nc.scalar.copy(out=out, in_=acc[:].rearrange("m q (n c) -> m q n c", c=HEAD_DIM))
+            nc.gpsimd.tensor_tensor(out=out, in0=out, in1=bias_of(s, n0), op=ALU.add)
+
+        def store(r, s, n0):
             dram = outs[s].rearrange("w n (h r q) c -> h r w n (q c)", h=2, r=ROUNDS)
-            for n0 in range(0, HEADS, PASS_HEADS):
-                cols = slice(n0 * HEAD_DIM, n0 * HEAD_DIM + PASS_COLS)
-                for q0 in range(0, ROW_LANES, BANK_LANES):
-                    acc = acc_psum.tile([P, BANK_LANES, PASS_COLS], F32, tag="acc")
-                    for e in range(BANK_LANES):
-                        rows = slice((q0 + e) * P, (q0 + e + 1) * P)
-                        nc.tensor.matmul_mx(
-                            out=acc[:, e, :],
-                            lhsT=s_codes[:, r, rows].bitcast(FP8X4),
-                            lhsT_scale=s_scales[:, r, rows],
-                            rhs=w_codes[:, s, cols].bitcast(FP8X4),
-                            rhs_scale=w_scales[:, s, cols],
-                            start=True,
-                            stop=True,
-                        )
-                    lane0 = r * ROW_LANES + q0
-                    nc.vector.tensor_tensor(
-                        out=out_sb[
-                            :, s, n0 : n0 + PASS_HEADS, lane0 : lane0 + BANK_LANES, :
-                        ].rearrange("m n q c -> m q n c"),
-                        in0=acc[:].rearrange("m q (n c) -> m q n c", c=HEAD_DIM),
-                        in1=bias_all[:, s, cols]
-                        .rearrange("m (o n c) -> m o n c", o=1, c=HEAD_DIM)
-                        .to_broadcast([P, BANK_LANES, PASS_HEADS, HEAD_DIM]),
-                        op=ALU.add,
-                    )
-                for half in range(2):
-                    nc.sync.dma_start(
-                        out=dram[half, r, :, n0 : n0 + PASS_HEADS, :],
-                        in_=out_sb[
-                            half:P:2,
-                            s,
-                            n0 : n0 + PASS_HEADS,
-                            r * ROW_LANES : (r + 1) * ROW_LANES,
-                            :,
-                        ].rearrange("m n q c -> m n (q c)"),
-                    )
+            for half in range(2):
+                nc.sync.dma_start(
+                    out=dram[half, r, :, n0 : n0 + PASS_HEADS, :],
+                    in_=out_sb[
+                        half:P:2,
+                        s,
+                        n0 : n0 + PASS_HEADS,
+                        r * ROW_LANES : (r + 1) * ROW_LANES,
+                        :,
+                    ].rearrange("m n q c -> m n (q c)"),
+                )
 
-        mean_var0 = row_moments(0)
-        nc.vector.tensor_copy(out=gain_cols[:, 0:PACK], in_=gain_raw[:])
-        nc.vector.tensor_copy(out=gain_cols[:, PACK : 2 * PACK], in_=bias_raw[:])
-        rstd0, shift0 = row_scales(mean_var0)
-        z_banks0 = normalise_and_transpose(0, rstd0, shift0)
-        rstd1, shift1 = row_scales(row_moments(1))
-        h_planes0 = gain_out_of_psum(z_banks0, vector_banks=2)
-        z_banks1 = normalise_and_transpose(1, rstd1, shift1)
-        w_grouped0 = regroup(nc.vector.tensor_copy, w_sb[:, 0, :, :], "w_grouped")
-        h_grouped0 = regroup(nc.vector.tensor_copy, h_planes0[:], "h_grouped")
-        quantise(w_grouped0, w_codes[:, 0, :], w_scales[:, 0, :])
-        w_grouped1 = regroup(nc.scalar.copy, w_sb[:, 1, :, :], "w_grouped")
-        quantise(h_grouped0, s_codes[:, 0, :], s_scales[:, 0, :])
-        quantise(w_grouped1, w_codes[:, 1, :], w_scales[:, 1, :])
-        w_grouped2 = regroup(nc.scalar.copy, w_sb[:, 2, :, :], "w_grouped")
-        h_planes1 = gain_out_of_psum(z_banks1, vector_banks=0)
-        h_grouped1 = regroup(nc.scalar.copy, h_planes1[:], "h_grouped")
-        project(0, 0)
-        quantise(w_grouped2, w_codes[:, 2, :], w_scales[:, 2, :])
-        project(0, 1)
-        quantise(h_grouped1, s_codes[:, 1, :], s_scales[:, 1, :])
-        project(0, 2)
-        for s in range(PARTS):
-            project(1, s)
+        H = PASS_HEADS
+        V, S, G = nc.vector, nc.scalar, nc.gpsimd
+        nc.gpsimd.tensor_copy(out=gain_cols[:, 0:PACK], in_=gain_raw[:])
+        nc.gpsimd.tensor_copy(out=gain_cols[:, PACK : 2 * PACK], in_=bias_raw[:])
+        row_stats(0)
+        row_stats(1)
+        neg_mean_on_scalar(3)
+        row_moments(0)
+        row_std(0)
+        dev_sum_on_scalar(3)
+        row_stats(2)
+        row_scales(0, False)
+        lane_moments(2)
+        lane_std(2, False)
+        lane_std(3, True)
+        z1 = normalise(1, V)
+        z0 = normalise(0, V)
+        zA = new_z_banks()
+        transpose(1, z1, zA)
+        transpose(0, z0, zA)
+        neg_mean_on_scalar(5)
+        row_scales(1, False)
+        z2 = normalise(2, V)
+        z3 = normalise(3, V, True)
+        regroup_w(V, 0, lo)
+        for t in range(4):
+            gain_out_of_psum(0, zA, t, S)
+        row_stats(4)
+        lane_moments(4)
+        zB = new_z_banks()
+        transpose(2, z2, zB)
+        transpose(3, z3, zB)
+        for t in range(4):
+            gain_out_of_psum(1, zB, t, S)
+        dev_sum_on_scalar(5)
+        regroup(V, h_planes[0][:], h_grouped[0][:])
+        quantise_w(0, lo)
+        quantise_h(0)
+        lane_std(4, False)
+        lane_std(5, True)
+        regroup_w(S, 0, hi)
+        regroup(V, h_planes[1][:], h_grouped[1][:])
+        row_scales(2, False)
+        quantise_h(1)
+        lane_shift(4)
+        lane_shift(5, True)
+        z4 = normalise(4, G)
+        z5 = normalise(5, G)
+        regroup_w(S, 1, lo)
+        vec(0, 0, 0)
+        quantise_w(0, hi)
+        vec(1, 0, 0)
+        store(0, 0, 0)
+        side(0, 0, H)
+        side(1, 0, H)
+        zC = new_z_banks()
+        transpose(4, z4, zC)
+        transpose(5, z5, zC)
+        quantise_w(1, lo)
+        row_stats(6)
+        row_stats(7)
+        regroup_w(S, 1, hi)
+        row_moments(3)
+        vec(0, 1, 0)
+        row_std(3)
+        for t in range(4):
+            gain_out_of_psum(2, zC, t, S)
+        vec(1, 1, 0)
+        store(0, 1, 0)
+        store(0, 0, H)
+        row_scales(3, True)
+        z6 = normalise(6, G)
+        z7 = normalise(7, G)
+        quantise_w(1, hi)
+        regroup_w(S, 2, lo)
+        regroup(V, h_planes[2][:], h_grouped[2][:])
+        vec(0, 1, H)
+        quantise_h(2)
+        vec(1, 1, H)
+        store(0, 1, H)
+        zD = new_z_banks()
+        transpose(6, z6, zD)
+        transpose(7, z7, zD)
+        for t in range(4):
+            gain_out_of_psum(3, zD, t, S)
+        side(2, 0, H)
+        quantise_w(2, lo)
+        vec(2, 0, 0)
+        regroup_w(S, 2, hi)
+        vec(0, 2, 0)
+        regroup(V, h_planes[3][:], h_grouped[3][:])
+        vec(1, 2, 0)
+        store(0, 2, 0)
+        quantise_h(3)
+        side(2, 1, H)
+        vec(2, 1, 0)
+        vec(3, 0, 0)
+        store(1, 0, 0)
+        side(3, 0, H)
+        quantise_w(2, hi)
+        vec(3, 1, 0)
+        store(1, 1, 0)
+        side(3, 1, H)
+        vec(0, 2, H)
+        store(1, 0, H)
+        vec(1, 2, H)
+        store(0, 2, H)
+        vec(2, 2, 0)
+        vec(3, 2, 0)
+        store(1, 2, 0)
+        store(1, 1, H)
+        vec(2, 2, H)
+        vec(3, 2, H)
+        store(1, 2, H)

@@ -423,68 +423,65 @@ def tile_swintransformerblock_pa_kernel(
         z4 = normalise(4, G)
         z5 = normalise(5, G)
         regroup_w(S, 1, lo)
+        for b in range(4):
+            regroup_w(G, 2, slice(b * P, (b + 1) * P))
         vec(0, 0, 0)
         quantise_w(0, hi)
         vec(1, 0, 0)
         store(0, 0, 0)
-        side(0, 0, H)
-        side(1, 0, H)
+        neg_mean_on_scalar(6)
+        dev_sum_on_scalar(6)
+        vec(0, 0, H)
+        regroup_w(S, 1, hi)
+        vec(1, 0, H)
+        store(0, 0, H)
         zC = new_z_banks()
         transpose(4, z4, zC)
         transpose(5, z5, zC)
         quantise_w(1, lo)
-        row_stats(6)
-        row_stats(7)
-        regroup_w(S, 1, hi)
-        row_moments(3)
-        vec(0, 1, 0)
-        row_std(3)
+        neg_mean_on_scalar(7)
+        dev_sum_on_scalar(7)
+        lane_std(6, True)
+        lane_std(7, True)
         for t in range(4):
             gain_out_of_psum(2, zC, t, S)
+        vec(0, 1, 0)
+        quantise_w(1, hi)
         vec(1, 1, 0)
         store(0, 1, 0)
-        store(0, 0, H)
-        row_scales(3, True)
+        row_scales(3, False)
+        lane_shift(6, True)
+        lane_shift(7, True)
         z6 = normalise(6, G)
         z7 = normalise(7, G)
-        quantise_w(1, hi)
-        regroup_w(S, 2, lo)
-        regroup(V, h_planes[2][:], h_grouped[2][:])
         vec(0, 1, H)
-        quantise_h(2)
+        quantise_w(2, lo)
         vec(1, 1, H)
         store(0, 1, H)
+        regroup(S, h_planes[2][:], h_grouped[2][:])
+        vec(0, 2, 0)
         zD = new_z_banks()
         transpose(6, z6, zD)
         transpose(7, z7, zD)
         for t in range(4):
             gain_out_of_psum(3, zD, t, S)
-        side(2, 0, H)
-        quantise_w(2, lo)
-        vec(2, 0, 0)
-        regroup_w(S, 2, hi)
-        vec(0, 2, 0)
-        regroup(V, h_planes[3][:], h_grouped[3][:])
+        quantise_w(2, hi)
         vec(1, 2, 0)
         store(0, 2, 0)
-        quantise_h(3)
-        side(2, 1, H)
-        vec(2, 1, 0)
-        vec(3, 0, 0)
-        store(1, 0, 0)
-        side(3, 0, H)
-        quantise_w(2, hi)
-        vec(3, 1, 0)
-        store(1, 1, 0)
-        side(3, 1, H)
+        quantise_h(2)
+        regroup(S, h_planes[3][:], h_grouped[3][:])
         vec(0, 2, H)
-        store(1, 0, H)
         vec(1, 2, H)
         store(0, 2, H)
-        vec(2, 2, 0)
-        vec(3, 2, 0)
-        store(1, 2, 0)
-        store(1, 1, H)
-        vec(2, 2, H)
-        vec(3, 2, H)
-        store(1, 2, H)
+        vec(2, 0, 0)
+        quantise_h(3)
+        vec(2, 0, H)
+        vec(3, 0, 0)
+        store(1, 0, 0)
+        vec(3, 0, H)
+        store(1, 0, H)
+        for s in (1, 2):
+            for n0 in (0, H):
+                vec(2, s, n0)
+                vec(3, s, n0)
+                store(1, s, n0)

@@ -48,6 +48,14 @@ def tile_swintransformerblock_pa_kernel(
         z_psum = ctx.enter_context(tc.psum_pool(name="z_psum", bufs=2))
         acc_psum = ctx.enter_context(tc.psum_pool(name="acc_psum", bufs=4))
 
+        zeros = const.tile([P, D], BF16)
+        nc.vector.memset(zeros[:], 0.0)
+        idle_bank = acc_psum.tile([P, D], F32, name="idle_bank", tag="acc")
+        for i in range(7):
+            nc.tensor.matmul(
+                out=idle_bank[:], lhsT=zeros[:, 0:P], rhs=zeros[:], start=True, stop=True
+            )
+
         x_sb = keep.tile([P, LANES, D], BF16)
         x_rows = x_win.rearrange("(i j) d -> i j d", j=LANES)
         w_sb = keep.tile([P, PARTS, PACK, D], BF16)
@@ -148,11 +156,11 @@ def tile_swintransformerblock_pa_kernel(
 
         neg_mean = [small.tile([P, 1], F32, name="neg_mean%d" % j) for j in range(LANES)]
         dev_sum = [small.tile([P, 1], F32, name="dev_sum%d" % j) for j in range(LANES)]
-        dump = keep.tile([P, D], BF16)
+        dump = [keep.tile([P, D], BF16, name="dump%d" % i) for i in range(2)]
 
         def neg_mean_on_scalar(lane):
             nc.scalar.activation(
-                out=dump[:],
+                out=dump[lane % 2][:],
                 in_=x_sb[:, lane, :],
                 func=ACT.Identity,
                 scale=-1.0 / D,
@@ -161,7 +169,7 @@ def tile_swintransformerblock_pa_kernel(
 
         def dev_sum_on_scalar(lane):
             nc.scalar.activation(
-                out=dump[:],
+                out=dump[lane % 2][:],
                 in_=x_sb[:, lane, :],
                 func=ACT.Square,
                 bias=neg_mean[lane][:],
@@ -312,22 +320,22 @@ def tile_swintransformerblock_pa_kernel(
         def quantise_w(s, cols):
             quantise(w_grouped[s][:, cols, :], w_codes[:, s, cols], w_scales[:, s, cols])
 
-        def group_out(s, n0, lane0):
+        def group_out(s, n0, heads, lane0):
             return out_sb[
-                :, s, n0 : n0 + PASS_HEADS, lane0 : lane0 + BANK_LANES, :
+                :, s, n0 : n0 + heads, lane0 : lane0 + BANK_LANES, :
             ].rearrange("m n q c -> m q n c")
 
-        def bias_of(s, n0):
+        def bias_of(s, n0, heads):
             return (
-                bias_all[:, s, n0 * HEAD_DIM : n0 * HEAD_DIM + PASS_COLS]
+                bias_all[:, s, n0 * HEAD_DIM : (n0 + heads) * HEAD_DIM]
                 .rearrange("m (o n c) -> m o n c", o=1, c=HEAD_DIM)
-                .to_broadcast([P, BANK_LANES, PASS_HEADS, HEAD_DIM])
+                .to_broadcast([P, BANK_LANES, heads, HEAD_DIM])
             )
 
-        def multiply(j, s, n0, pool, tag):
+        def multiply(j, s, n0, heads, pool, tag):
             r, rows0 = pair_cols(j)
-            cols = slice(n0 * HEAD_DIM, n0 * HEAD_DIM + PASS_COLS)
-            acc = pool.tile([P, BANK_LANES, PASS_COLS], F32, name="acc", tag=tag)
+            cols = slice(n0 * HEAD_DIM, (n0 + heads) * HEAD_DIM)
+            acc = pool.tile([P, BANK_LANES, heads * HEAD_DIM], F32, name="acc", tag=tag)
             for e in range(BANK_LANES):
                 rows = slice(rows0.start + e * P, rows0.start + (e + 1) * P)
                 nc.tensor.matmul_mx(
@@ -341,34 +349,28 @@ def tile_swintransformerblock_pa_kernel(
                 )
             return acc
 
-        def out_of_bank(j, s, n0):
+        def out_of_bank(j, s, n0, heads):
             r, rows0 = pair_cols(j)
-            return group_out(s, n0, r * ROW_LANES + rows0.start // P)
+            return group_out(s, n0, heads, r * ROW_LANES + rows0.start // P)
 
-        def vec(j, s, n0):
-            acc = multiply(j, s, n0, acc_psum, "acc")
+        def vec(j, s, n0, heads=PASS_HEADS):
+            acc = multiply(j, s, n0, heads, acc_psum, "acc")
             nc.vector.tensor_tensor(
-                out=out_of_bank(j, s, n0),
+                out=out_of_bank(j, s, n0, heads),
                 in0=acc[:].rearrange("m q (n c) -> m q n c", c=HEAD_DIM),
-                in1=bias_of(s, n0),
+                in1=bias_of(s, n0, heads),
                 op=ALU.add,
             )
 
-        def side(j, s, n0):
-            acc = multiply(j, s, n0, z_psum, "z_bank%d" % (j % 2))
-            out = out_of_bank(j, s, n0)
-            nc.scalar.copy(out=out, in_=acc[:].rearrange("m q (n c) -> m q n c", c=HEAD_DIM))
-            nc.gpsimd.tensor_tensor(out=out, in0=out, in1=bias_of(s, n0), op=ALU.add)
-
-        def store(r, s, n0):
+        def store(r, s, n0, heads=PASS_HEADS):
             dram = outs[s].rearrange("w n (h r q) c -> h r w n (q c)", h=2, r=ROUNDS)
             for half in range(2):
                 nc.sync.dma_start(
-                    out=dram[half, r, :, n0 : n0 + PASS_HEADS, :],
+                    out=dram[half, r, :, n0 : n0 + heads, :],
                     in_=out_sb[
                         half:P:2,
                         s,
-                        n0 : n0 + PASS_HEADS,
+                        n0 : n0 + heads,
                         r * ROW_LANES : (r + 1) * ROW_LANES,
                         :,
                     ].rearrange("m n q c -> m n (q c)"),
@@ -394,32 +396,31 @@ def tile_swintransformerblock_pa_kernel(
         zA = new_z_banks()
         transpose(1, z1, zA)
         transpose(0, z0, zA)
-        neg_mean_on_scalar(5)
+        regroup_w(S, 0, lo)
         row_scales(1, False)
         z2 = normalise(2, V)
         z3 = normalise(3, V, True)
-        regroup_w(V, 0, lo)
         for t in range(4):
             gain_out_of_psum(0, zA, t, S)
         row_stats(4)
-        lane_moments(4)
+        row_stats(5)
+        row_moments(2)
         zB = new_z_banks()
         transpose(2, z2, zB)
         transpose(3, z3, zB)
         for t in range(4):
             gain_out_of_psum(1, zB, t, S)
-        dev_sum_on_scalar(5)
         regroup(V, h_planes[0][:], h_grouped[0][:])
         quantise_w(0, lo)
         quantise_h(0)
-        lane_std(4, False)
-        lane_std(5, True)
+        row_std(2)
         regroup_w(S, 0, hi)
         regroup(V, h_planes[1][:], h_grouped[1][:])
-        row_scales(2, False)
+        lane_rstd(4)
+        lane_rstd(5)
         quantise_h(1)
         lane_shift(4)
-        lane_shift(5, True)
+        lane_shift(5)
         z4 = normalise(4, G)
         z5 = normalise(5, G)
         regroup_w(S, 1, lo)
@@ -429,17 +430,17 @@ def tile_swintransformerblock_pa_kernel(
         quantise_w(0, hi)
         vec(1, 0, 0)
         store(0, 0, 0)
-        neg_mean_on_scalar(6)
-        dev_sum_on_scalar(6)
-        vec(0, 0, H)
         regroup_w(S, 1, hi)
+        vec(0, 0, H)
+        quantise_w(1, lo)
         vec(1, 0, H)
         store(0, 0, H)
         zC = new_z_banks()
         transpose(4, z4, zC)
         transpose(5, z5, zC)
-        quantise_w(1, lo)
+        neg_mean_on_scalar(6)
         neg_mean_on_scalar(7)
+        dev_sum_on_scalar(6)
         dev_sum_on_scalar(7)
         lane_std(6, True)
         lane_std(7, True)
@@ -454,34 +455,41 @@ def tile_swintransformerblock_pa_kernel(
         lane_shift(7, True)
         z6 = normalise(6, G)
         z7 = normalise(7, G)
+        regroup(S, h_planes[2][:], h_grouped[2][:])
         vec(0, 1, H)
-        quantise_w(2, lo)
+        quantise_w(2, full)
         vec(1, 1, H)
         store(0, 1, H)
-        regroup(S, h_planes[2][:], h_grouped[2][:])
         vec(0, 2, 0)
+        vec(1, 2, 0)
+        store(0, 2, 0)
         zD = new_z_banks()
         transpose(6, z6, zD)
         transpose(7, z7, zD)
         for t in range(4):
             gain_out_of_psum(3, zD, t, S)
-        quantise_w(2, hi)
-        vec(1, 2, 0)
-        store(0, 2, 0)
-        quantise_h(2)
         regroup(S, h_planes[3][:], h_grouped[3][:])
         vec(0, 2, H)
+        quantise_h(2)
         vec(1, 2, H)
         store(0, 2, H)
         vec(2, 0, 0)
-        quantise_h(3)
         vec(2, 0, H)
+        quantise_h(3)
+        vec(2, 1, 0)
         vec(3, 0, 0)
         store(1, 0, 0)
         vec(3, 0, H)
         store(1, 0, H)
-        for s in (1, 2):
-            for n0 in (0, H):
-                vec(2, s, n0)
-                vec(3, s, n0)
-                store(1, s, n0)
+        vec(3, 1, 0)
+        store(1, 1, 0)
+        vec(2, 1, H)
+        vec(3, 1, H)
+        store(1, 1, H)
+        vec(2, 2, 0)
+        vec(3, 2, 0)
+        store(1, 2, 0)
+        for n0 in (H, H + 2):
+            vec(2, 2, n0, 2)
+            vec(3, 2, n0, 2)
+            store(1, 2, n0, 2)

@@ -416,76 +416,76 @@ def tile_swintransformerblock_pa_kernel(
         row_std(2)
         regroup_w(S, 0, hi)
         regroup(V, h_planes[1][:], h_grouped[1][:])
+        regroup_w(S, 1, lo)
         lane_rstd(4)
         lane_rstd(5)
         quantise_h(1)
+        quantise_w(0, hi)
         lane_shift(4)
         lane_shift(5)
         z4 = normalise(4, G)
         z5 = normalise(5, G)
-        regroup_w(S, 1, lo)
-        for b in range(4):
-            regroup_w(G, 2, slice(b * P, (b + 1) * P))
         vec(0, 0, 0)
-        quantise_w(0, hi)
+        regroup_w(S, 1, hi)
         vec(1, 0, 0)
         store(0, 0, 0)
-        regroup_w(S, 1, hi)
+        row_stats(6)
+        neg_mean_on_scalar(7)
+        dev_sum_on_scalar(7)
+        lane_moments(6)
         vec(0, 0, H)
         quantise_w(1, lo)
-        vec(1, 0, H)
-        store(0, 0, H)
+        quantise_w(1, hi)
+        lane_std(7, True)
+        lane_std(6, False)
+        regroup_w(S, 2, lo)
         zC = new_z_banks()
         transpose(4, z4, zC)
         transpose(5, z5, zC)
-        neg_mean_on_scalar(6)
-        neg_mean_on_scalar(7)
-        dev_sum_on_scalar(6)
-        dev_sum_on_scalar(7)
-        lane_std(6, True)
-        lane_std(7, True)
-        for t in range(4):
-            gain_out_of_psum(2, zC, t, S)
+        vec(1, 0, H)
+        store(0, 0, H)
+        lane_rstd(6)
+        lane_rstd(7)
         vec(0, 1, 0)
-        quantise_w(1, hi)
-        vec(1, 1, 0)
-        store(0, 1, 0)
-        row_scales(3, False)
-        lane_shift(6, True)
+        lane_shift(6)
         lane_shift(7, True)
         z6 = normalise(6, G)
         z7 = normalise(7, G)
+        vec(1, 1, 0)
+        store(0, 1, 0)
+        regroup_w(S, 2, hi)
+        for t in range(4):
+            gain_out_of_psum(2, zC, t, S)
         regroup(S, h_planes[2][:], h_grouped[2][:])
         vec(0, 1, H)
-        quantise_w(2, full)
         vec(1, 1, H)
         store(0, 1, H)
-        vec(0, 2, 0)
-        vec(1, 2, 0)
-        store(0, 2, 0)
         zD = new_z_banks()
         transpose(6, z6, zD)
         transpose(7, z7, zD)
         for t in range(4):
             gain_out_of_psum(3, zD, t, S)
         regroup(S, h_planes[3][:], h_grouped[3][:])
-        vec(0, 2, H)
+        quantise_w(2, lo)
+        quantise_w(2, hi)
+        vec(0, 2, 0)
+        vec(1, 2, 0)
+        store(0, 2, 0)
         quantise_h(2)
+        vec(0, 2, H)
         vec(1, 2, H)
         store(0, 2, H)
         vec(2, 0, 0)
-        vec(2, 0, H)
         quantise_h(3)
-        vec(2, 1, 0)
+        vec(2, 0, H)
         vec(3, 0, 0)
         store(1, 0, 0)
         vec(3, 0, H)
         store(1, 0, H)
-        vec(3, 1, 0)
-        store(1, 1, 0)
-        vec(2, 1, H)
-        vec(3, 1, H)
-        store(1, 1, H)
+        for n0 in (0, H):
+            vec(2, 1, n0)
+            vec(3, 1, n0)
+            store(1, 1, n0)
         vec(2, 2, 0)
         vec(3, 2, 0)
         store(1, 2, 0)

@@ -314,8 +314,11 @@ def tile_swintransformerblock_pa_kernel(
         hi = slice(PASS_COLS, D)
         full = slice(0, D)
 
-        def regroup_w(engine, s, cols):
-            regroup(engine, w_sb[:, s, :, cols], w_grouped[s][:, cols, :])
+        def regroup_w(engine, s, cols, pieces=1):
+            width = (cols.stop - cols.start) // pieces
+            for c0 in range(cols.start, cols.stop, width):
+                part = slice(c0, c0 + width)
+                regroup(engine, w_sb[:, s, :, part], w_grouped[s][:, part, :])
 
         def quantise_w(s, cols):
             quantise(w_grouped[s][:, cols, :], w_codes[:, s, cols], w_scales[:, s, cols])
@@ -376,6 +379,14 @@ def tile_swintransformerblock_pa_kernel(
                     ].rearrange("m n q c -> m n (q c)"),
                 )
 
+        def store_both(s, n0, heads):
+            dram = outs[s].rearrange("w n (h p) c -> h w n (p c)", h=2)
+            for half in range(2):
+                nc.sync.dma_start(
+                    out=dram[half, :, n0 : n0 + heads, :],
+                    in_=out_sb[half:P:2, s, n0 : n0 + heads, :, :].rearrange("m n p c -> m n (p c)"),
+                )
+
         H = PASS_HEADS
         V, S, G = nc.vector, nc.scalar, nc.gpsimd
         nc.gpsimd.tensor_copy(out=gain_cols[:, 0:PACK], in_=gain_raw[:])
@@ -425,6 +436,7 @@ def tile_swintransformerblock_pa_kernel(
         lane_shift(5)
         z4 = normalise(4, G)
         z5 = normalise(5, G)
+        regroup_w(G, 2, lo, 2)
         vec(0, 0, 0)
         regroup_w(S, 1, hi)
         vec(1, 0, 0)
@@ -432,47 +444,46 @@ def tile_swintransformerblock_pa_kernel(
         row_stats(6)
         neg_mean_on_scalar(7)
         dev_sum_on_scalar(7)
-        lane_moments(6)
         vec(0, 0, H)
-        quantise_w(1, lo)
-        quantise_w(1, hi)
+        lane_moments(6)
+        vec(1, 0, H)
+        store(0, 0, H)
         lane_std(7, True)
         lane_std(6, False)
-        regroup_w(S, 2, lo)
+        quantise_w(1, lo)
+        quantise_w(1, hi)
+        quantise_w(2, lo)
+        lane_rstd(6)
+        lane_rstd(7)
         zC = new_z_banks()
         transpose(4, z4, zC)
         transpose(5, z5, zC)
-        vec(1, 0, H)
-        store(0, 0, H)
-        lane_rstd(6)
-        lane_rstd(7)
+        for t in range(4):
+            gain_out_of_psum(2, zC, t, S)
         vec(0, 1, 0)
         lane_shift(6)
         lane_shift(7, True)
         z6 = normalise(6, G)
         z7 = normalise(7, G)
+        regroup_w(S, 2, hi)
         vec(1, 1, 0)
         store(0, 1, 0)
-        regroup_w(S, 2, hi)
-        for t in range(4):
-            gain_out_of_psum(2, zC, t, S)
-        regroup(S, h_planes[2][:], h_grouped[2][:])
         vec(0, 1, H)
         vec(1, 1, H)
         store(0, 1, H)
+        regroup(S, h_planes[2][:], h_grouped[2][:])
+        vec(0, 2, 0)
+        quantise_w(2, hi)
+        vec(1, 2, 0)
+        store(0, 2, 0)
         zD = new_z_banks()
         transpose(6, z6, zD)
         transpose(7, z7, zD)
         for t in range(4):
             gain_out_of_psum(3, zD, t, S)
         regroup(S, h_planes[3][:], h_grouped[3][:])
-        quantise_w(2, lo)
-        quantise_w(2, hi)
-        vec(0, 2, 0)
-        vec(1, 2, 0)
-        store(0, 2, 0)
-        quantise_h(2)
         vec(0, 2, H)
+        quantise_h(2)
         vec(1, 2, H)
         store(0, 2, H)
         vec(2, 0, 0)

@@ -154,17 +154,16 @@ def tile_swintransformerblock_pa_kernel(
             for lane in range(PAIR * j, PAIR * j + PAIR):
                 nc.vector.bn_aggr(out=mean_var[:, lane, :], in_=stats[:, lane, :])
 
-        neg_mean = [small.tile([P, 1], F32, name="neg_mean%d" % j) for j in range(LANES)]
         dev_sum = [small.tile([P, 1], F32, name="dev_sum%d" % j) for j in range(LANES)]
         dump = [keep.tile([P, D], BF16, name="dump%d" % i) for i in range(2)]
 
-        def neg_mean_on_scalar(lane):
+        def mean_on_scalar(lane):
             nc.scalar.activation(
                 out=dump[lane % 2][:],
                 in_=x_sb[:, lane, :],
                 func=ACT.Identity,
-                scale=-1.0 / D,
-                accum_out=neg_mean[lane][:],
+                scale=1.0 / D,
+                accum_out=mean_var[:, lane, 0:1],
             )
 
         def dev_sum_on_scalar(lane):
@@ -172,7 +171,8 @@ def tile_swintransformerblock_pa_kernel(
                 out=dump[lane % 2][:],
                 in_=x_sb[:, lane, :],
                 func=ACT.Square,
-                bias=neg_mean[lane][:],
+                scale=-1.0,
+                bias=mean_var[:, lane, 0:1],
                 accum_out=dev_sum[lane][:],
             )
 
@@ -197,34 +197,20 @@ def tile_swintransformerblock_pa_kernel(
                 bias=eps[:],
             )
 
-        def row_scales(j, with_shift):
+        def pair_rstd(j):
             nc.vector.reciprocal(out=rstd[j][:], in_=std[j][:])
-            if with_shift:
-                nc.vector.scalar_tensor_tensor(
-                    out=shift[j][:],
-                    in0=mean_var[:, PAIR * j : PAIR * j + PAIR, 0],
-                    scalar=-1.0,
-                    in1=rstd[j][:],
-                    op0=ALU.mult,
-                    op1=ALU.mult,
-                )
 
-        def lane_rstd(lane):
-            j, e = divmod(lane, PAIR)
-            nc.vector.reciprocal(out=rstd[j][:, e : e + 1], in_=std[j][:, e : e + 1])
-
-        def lane_shift(lane, from_scalar=False):
-            j, e = divmod(lane, PAIR)
+        def pair_shift(j):
             nc.vector.scalar_tensor_tensor(
-                out=shift[j][:, e : e + 1],
-                in0=neg_mean[lane][:] if from_scalar else mean_var[:, lane, 0:1],
-                scalar=1.0 if from_scalar else -1.0,
-                in1=rstd[j][:, e : e + 1],
+                out=shift[j][:],
+                in0=mean_var[:, PAIR * j : PAIR * j + PAIR, 0],
+                scalar=-1.0,
+                in1=rstd[j][:],
                 op0=ALU.mult,
                 op1=ALU.mult,
             )
 
-        def normalise(lane, engine, from_scalar=False):
+        def normalise(lane, engine):
             z = z_pool.tile([P, D], F32)
             z_out = z[:].rearrange("i (t p) -> i t p", t=PACK)
             x_in = x_sb[:, lane, :].rearrange("i (p t) -> i t p", t=PACK)
@@ -241,9 +227,9 @@ def tile_swintransformerblock_pa_kernel(
                 nc.vector.tensor_scalar(
                     out=z_out,
                     in0=x_in,
-                    scalar1=neg_mean[lane][:] if from_scalar else mean_var[:, lane, 0:1],
+                    scalar1=mean_var[:, lane, 0:1],
                     scalar2=rstd[j][:, e : e + 1],
-                    op0=ALU.add if from_scalar else ALU.subtract,
+                    op0=ALU.subtract,
                     op1=ALU.mult,
                 )
             else:
@@ -368,7 +354,8 @@ def tile_swintransformerblock_pa_kernel(
         def store(r, s, n0, heads=PASS_HEADS):
             dram = outs[s].rearrange("w n (h r q) c -> h r w n (q c)", h=2, r=ROUNDS)
             for half in range(2):
-                nc.sync.dma_start(
+                queue = nc.scalar if r == 1 and half == 1 else nc.sync
+                queue.dma_start(
                     out=dram[half, r, :, n0 : n0 + heads, :],
                     in_=out_sb[
                         half:P:2,
@@ -393,12 +380,12 @@ def tile_swintransformerblock_pa_kernel(
         nc.gpsimd.tensor_copy(out=gain_cols[:, PACK : 2 * PACK], in_=bias_raw[:])
         row_stats(0)
         row_stats(1)
-        neg_mean_on_scalar(3)
+        mean_on_scalar(3)
         row_moments(0)
         row_std(0)
         dev_sum_on_scalar(3)
         row_stats(2)
-        row_scales(0, False)
+        pair_rstd(0)
         lane_moments(2)
         lane_std(2, False)
         lane_std(3, True)
@@ -408,9 +395,9 @@ def tile_swintransformerblock_pa_kernel(
         transpose(1, z1, zA)
         transpose(0, z0, zA)
         regroup_w(S, 0, lo)
-        row_scales(1, False)
+        pair_rstd(1)
         z2 = normalise(2, V)
-        z3 = normalise(3, V, True)
+        z3 = normalise(3, V)
         for t in range(4):
             gain_out_of_psum(0, zA, t, S)
         row_stats(4)
@@ -428,43 +415,38 @@ def tile_swintransformerblock_pa_kernel(
         regroup_w(S, 0, hi)
         regroup(V, h_planes[1][:], h_grouped[1][:])
         regroup_w(S, 1, lo)
-        lane_rstd(4)
-        lane_rstd(5)
+        pair_rstd(2)
         quantise_h(1)
         quantise_w(0, hi)
-        lane_shift(4)
-        lane_shift(5)
+        pair_shift(2)
         z4 = normalise(4, G)
         z5 = normalise(5, G)
-        regroup_w(G, 2, lo, 2)
         vec(0, 0, 0)
         regroup_w(S, 1, hi)
         vec(1, 0, 0)
         store(0, 0, 0)
         row_stats(6)
-        neg_mean_on_scalar(7)
+        mean_on_scalar(7)
         dev_sum_on_scalar(7)
         vec(0, 0, H)
         lane_moments(6)
+        quantise_w(1, lo)
         vec(1, 0, H)
         store(0, 0, H)
         lane_std(7, True)
         lane_std(6, False)
-        quantise_w(1, lo)
         quantise_w(1, hi)
-        quantise_w(2, lo)
-        lane_rstd(6)
-        lane_rstd(7)
+        pair_rstd(3)
         zC = new_z_banks()
         transpose(4, z4, zC)
         transpose(5, z5, zC)
         for t in range(4):
             gain_out_of_psum(2, zC, t, S)
         vec(0, 1, 0)
-        lane_shift(6)
-        lane_shift(7, True)
+        pair_shift(3)
         z6 = normalise(6, G)
         z7 = normalise(7, G)
+        regroup_w(S, 2, lo)
         regroup_w(S, 2, hi)
         vec(1, 1, 0)
         store(0, 1, 0)
@@ -472,16 +454,17 @@ def tile_swintransformerblock_pa_kernel(
         vec(1, 1, H)
         store(0, 1, H)
         regroup(S, h_planes[2][:], h_grouped[2][:])
-        vec(0, 2, 0)
-        quantise_w(2, hi)
-        vec(1, 2, 0)
-        store(0, 2, 0)
         zD = new_z_banks()
         transpose(6, z6, zD)
         transpose(7, z7, zD)
         for t in range(4):
             gain_out_of_psum(3, zD, t, S)
         regroup(S, h_planes[3][:], h_grouped[3][:])
+        quantise_w(2, lo)
+        quantise_w(2, hi)
+        vec(0, 2, 0)
+        vec(1, 2, 0)
+        store(0, 2, 0)
         vec(0, 2, H)
         quantise_h(2)
         vec(1, 2, H)

@@ -50,11 +50,15 @@ def tile_swintransformerblock_pa_kernel(
 
         zeros = const.tile([P, D], BF16)
         nc.vector.memset(zeros[:], 0.0)
-        idle_bank = acc_psum.tile([P, D], F32, name="idle_bank", tag="acc")
-        for i in range(7):
-            nc.tensor.matmul(
-                out=idle_bank[:], lhsT=zeros[:, 0:P], rhs=zeros[:], start=True, stop=True
-            )
+
+        def idle_passes(count):
+            idle_bank = acc_psum.tile([P, D], F32, name="idle_bank", tag="acc")
+            for i in range(count):
+                nc.tensor.matmul(
+                    out=idle_bank[:], lhsT=zeros[:, 0:P], rhs=zeros[:], start=True, stop=True
+                )
+
+        idle_passes(7)
 
         x_sb = keep.tile([P, LANES, D], BF16)
         x_rows = x_win.rearrange("(i j) d -> i j d", j=LANES)
@@ -354,8 +358,7 @@ def tile_swintransformerblock_pa_kernel(
         def store(r, s, n0, heads=PASS_HEADS):
             dram = outs[s].rearrange("w n (h r q) c -> h r w n (q c)", h=2, r=ROUNDS)
             for half in range(2):
-                queue = nc.scalar if r == 1 and half == 1 else nc.sync
-                queue.dma_start(
+                nc.sync.dma_start(
                     out=dram[half, r, :, n0 : n0 + heads, :],
                     in_=out_sb[
                         half:P:2,
@@ -406,6 +409,7 @@ def tile_swintransformerblock_pa_kernel(
         zB = new_z_banks()
         transpose(2, z2, zB)
         transpose(3, z3, zB)
+        idle_passes(2)
         for t in range(4):
             gain_out_of_psum(1, zB, t, S)
         regroup(V, h_planes[0][:], h_grouped[0][:])
@@ -422,51 +426,51 @@ def tile_swintransformerblock_pa_kernel(
         z4 = normalise(4, G)
         z5 = normalise(5, G)
         vec(0, 0, 0)
+        mean_on_scalar(7)
         regroup_w(S, 1, hi)
+        dev_sum_on_scalar(7)
         vec(1, 0, 0)
         store(0, 0, 0)
         row_stats(6)
-        mean_on_scalar(7)
-        dev_sum_on_scalar(7)
         vec(0, 0, H)
         lane_moments(6)
         quantise_w(1, lo)
         vec(1, 0, H)
         store(0, 0, H)
-        lane_std(7, True)
         lane_std(6, False)
-        quantise_w(1, hi)
+        lane_std(7, True)
         pair_rstd(3)
-        zC = new_z_banks()
-        transpose(4, z4, zC)
-        transpose(5, z5, zC)
-        for t in range(4):
-            gain_out_of_psum(2, zC, t, S)
-        vec(0, 1, 0)
+        quantise_w(1, hi)
         pair_shift(3)
         z6 = normalise(6, G)
         z7 = normalise(7, G)
+        zC = new_z_banks()
+        transpose(4, z4, zC)
+        transpose(5, z5, zC)
         regroup_w(S, 2, lo)
-        regroup_w(S, 2, hi)
+        for t in range(4):
+            gain_out_of_psum(2, zC, t, S)
+        vec(0, 1, 0)
         vec(1, 1, 0)
         store(0, 1, 0)
         vec(0, 1, H)
+        quantise_w(2, lo)
+        regroup_w(S, 2, hi)
         vec(1, 1, H)
         store(0, 1, H)
         regroup(S, h_planes[2][:], h_grouped[2][:])
+        vec(0, 2, 0)
         zD = new_z_banks()
         transpose(6, z6, zD)
         transpose(7, z7, zD)
         for t in range(4):
             gain_out_of_psum(3, zD, t, S)
         regroup(S, h_planes[3][:], h_grouped[3][:])
-        quantise_w(2, lo)
         quantise_w(2, hi)
-        vec(0, 2, 0)
         vec(1, 2, 0)
         store(0, 2, 0)
-        vec(0, 2, H)
         quantise_h(2)
+        vec(0, 2, H)
         vec(1, 2, H)
         store(0, 2, H)
         vec(2, 0, 0)

from contextlib import ExitStack

import concourse.mybir as mybir
from concourse.masks import make_identity

F32 = mybir.dt.float32
BF16 = mybir.dt.bfloat16
U32 = mybir.dt.uint32
U8 = mybir.dt.uint8
FP8X4 = mybir.dt.float8_e4m3fn_x4
ACT = mybir.ActivationFunctionType
ALU = mybir.AluOpType

P = 128
PACK = 4
D = P * PACK
GRID = 8
WINDOWS = GRID * GRID
LANES = 8
ROW_LANES = 4
ROUNDS = LANES // ROW_LANES
PARTS = 3
HEADS = 8
HEAD_DIM = D // HEADS
PASS_HEADS = 4
PASS_COLS = PASS_HEADS * HEAD_DIM
BANK_LANES = 2
LOAD_LANES = 2
PAIR = 2
EPS = 1e-5

FLOPS = 2 * (P * LANES) * D * (PARTS * D)


def tile_swintransformerblock_pa_kernel(
    tc, x_win, ln3_g, ln3_b, qkv2_w, qkv2_b, out_0, out_1, out_2
):
    nc = tc.nc
    outs = (out_0, out_1, out_2)

    with ExitStack() as ctx:
        ctx.enter_context(tc.manual_schedule())
        const = ctx.enter_context(tc.tile_pool(name="const", bufs=1))
        keep = ctx.enter_context(tc.tile_pool(name="keep", bufs=1))
        small = ctx.enter_context(tc.tile_pool(name="small", bufs=1))
        z_pool = ctx.enter_context(tc.tile_pool(name="z_pool", bufs=4))
        stage = ctx.enter_context(tc.tile_pool(name="stage", bufs=1))
        z_psum = ctx.enter_context(tc.psum_pool(name="z_psum", bufs=2))
        acc_psum = ctx.enter_context(tc.psum_pool(name="acc_psum", bufs=4))

        zeros = const.tile([P, D], BF16)
        nc.vector.memset(zeros[:], 0.0)

        def idle_passes(count):
            idle_bank = acc_psum.tile([P, D], F32, name="idle_bank", tag="acc")
            for i in range(count):
                nc.tensor.matmul(
                    out=idle_bank[:], lhsT=zeros[:, 0:P], rhs=zeros[:], start=True, stop=True
                )

        idle_passes(7)

        x_sb = keep.tile([P, LANES, D], BF16)
        x_rows = x_win.rearrange("(i j) d -> i j d", j=LANES)
        w_sb = keep.tile([P, PARTS, PACK, D], BF16)
        w_rows = qkv2_w.rearrange("(p t) (s n) -> p s t n", p=P, s=PARTS)
        gain_raw = const.tile([P, PACK], BF16)
        bias_raw = const.tile([P, PACK], BF16)
        bias_all = const.tile([P, PARTS, D], BF16)

        def load_x(lane0, lanes=LOAD_LANES):
            lanes = slice(lane0, lane0 + lanes)
            nc.sync.dma_start(out=x_sb[:, lanes, :], in_=x_rows[:, lanes, :])

        def load_w(s):
            nc.sync.dma_start(out=w_sb[:, s, :, :], in_=w_rows[:, s, :, :])

        load_x(0, 1)
        load_x(1, 1)
        load_x(LOAD_LANES)
        load_w(0)
        nc.sync.dma_start(out=gain_raw[:], in_=ln3_g.rearrange("(p t) -> p t", p=P))
        nc.sync.dma_start(out=bias_raw[:], in_=ln3_b.rearrange("(p t) -> p t", p=P))
        load_x(2 * LOAD_LANES)
        load_x(3 * LOAD_LANES)
        load_w(1)
        nc.sync.dma_start(
            out=bias_all[:].rearrange("m s n -> m (s n)"), in_=qkv2_b.partition_broadcast(P)
        )
        load_w(2)

        eps = const.tile([P, 1], F32)
        nc.vector.memset(eps[:], EPS)
        table_warmer = const.tile([P, 1], F32)
        nc.scalar.activation(out=table_warmer[:], in_=eps[:], func=ACT.Sqrt)

        ident = const.tile([P, P], F32)
        make_identity(nc, ident[:])

        take_below = const.tile([P, P], F32)
        from_half = ident[:].rearrange("i (w h) -> i w h", h=2)
        to_half = take_below[:].rearrange("i (w h) -> i w h", h=2)
        nc.vector.tensor_copy(out=to_half[:, :, 0], in_=from_half[:, :, 1])
        nc.vector.tensor_copy(
            out=to_half[:, 0 : WINDOWS - GRID, 1], in_=from_half[:, GRID:WINDOWS, 0]
        )
        nc.vector.tensor_copy(
            out=to_half[:, WINDOWS - GRID : WINDOWS, 1], in_=from_half[:, 0:GRID, 0]
        )
        take_below_right = const.tile([P, P], F32)
        from_row = take_below[:].rearrange("i (r e) -> i r e", e=2 * GRID)
        to_row = take_below_right[:].rearrange("i (r e) -> i r e", e=2 * GRID)
        nc.vector.tensor_copy(out=to_row[:, :, 0 : 2 * GRID - 2], in_=from_row[:, :, 2 : 2 * GRID])
        nc.vector.tensor_copy(out=to_row[:, :, 2 * GRID - 2 : 2 * GRID], in_=from_row[:, :, 0:2])

        s_codes = keep.tile([P, ROUNDS, ROW_LANES * P], U32, align_bytes=64)
        s_scales = keep.tile([P, ROUNDS, ROW_LANES * P], U8, align_bytes=64)
        w_codes = keep.tile([P, PARTS, D], U32, align_bytes=64)
        w_scales = keep.tile([P, PARTS, D], U8, align_bytes=64)
        out_sb = keep.tile([P, PARTS, HEADS, LANES, HEAD_DIM], F32)

        gain_cols = const.tile([P, 2 * PACK], F32)

        def regroup(engine, planes, grouped):
            if engine is nc.gpsimd:
                nc.gpsimd.tensor_scalar(
                    out=grouped,
                    in0=planes.rearrange("p t c -> p c t"),
                    scalar1=1.0,
                    scalar2=0.0,
                    op0=ALU.mult,
                    op1=ALU.add,
                )
                return
            copy = nc.scalar.copy if engine is nc.scalar else nc.vector.tensor_copy
            copy(
                out=grouped.rearrange("p (c i) t -> p c t i", i=4),
                in_=planes.rearrange("p t (c i) -> p c t i", i=4),
            )

        def quantise(grouped, codes, scales):
            nc.vector.quantize_mx(
                out=codes.bitcast(FP8X4),
                scales=scales,
                in_=grouped.rearrange("p c t -> p (c t)"),
            )

        stats = keep.tile([P, LANES, 6], F32)
        mean_var = keep.tile([P, LANES, 2], F32)
        std = [small.tile([P, PAIR], F32, name="std%d" % j) for j in range(LANES // PAIR)]
        rstd = [small.tile([P, PAIR], F32, name="rstd%d" % j) for j in range(LANES // PAIR)]
        shift = [small.tile([P, PAIR], F32, name="shift%d" % j) for j in range(LANES // PAIR)]

        def row_stats(lane):
            nc.vector.bn_stats(out=stats[:, lane, :], in_=x_sb[:, lane, :])

        def row_moments(j):
            for lane in range(PAIR * j, PAIR * j + PAIR):
                nc.vector.bn_aggr(out=mean_var[:, lane, :], in_=stats[:, lane, :])

        dev_sum = [small.tile([P, 1], F32, name="dev_sum%d" % j) for j in range(LANES)]
        dump = [keep.tile([P, D], BF16, name="dump%d" % i) for i in range(2)]

        def mean_on_scalar(lane):
            nc.scalar.activation(
                out=dump[lane % 2][:],
                in_=x_sb[:, lane, :],
                func=ACT.Identity,
                scale=1.0 / D,
                accum_out=mean_var[:, lane, 0:1],
            )

        def dev_sum_on_scalar(lane):
            nc.scalar.activation(
                out=dump[lane % 2][:],
                in_=x_sb[:, lane, :],
                func=ACT.Square,
                scale=-1.0,
                bias=mean_var[:, lane, 0:1],
                accum_out=dev_sum[lane][:],
            )

        def lane_std(lane, from_scalar):
            j, e = divmod(lane, PAIR)
            nc.scalar.activation(
                out=std[j][:, e : e + 1],
                in_=dev_sum[lane][:] if from_scalar else mean_var[:, lane, 1:2],
                func=ACT.Sqrt,
                bias=eps[:],
                scale=1.0 / D if from_scalar else 1.0,
            )

        def lane_moments(lane):
            nc.vector.bn_aggr(out=mean_var[:, lane, :], in_=stats[:, lane, :])

        def row_std(j):
            nc.scalar.activation(
                out=std[j][:],
                in_=mean_var[:, PAIR * j : PAIR * j + PAIR, 1],
                func=ACT.Sqrt,
                bias=eps[:],
            )

        def pair_rstd(j):
            nc.vector.reciprocal(out=rstd[j][:], in_=std[j][:])

        def pair_shift(j):
            nc.vector.scalar_tensor_tensor(
                out=shift[j][:],
                in0=mean_var[:, PAIR * j : PAIR * j + PAIR, 0],
                scalar=-1.0,
                in1=rstd[j][:],
                op0=ALU.mult,
                op1=ALU.mult,
            )

        def normalise(lane, engine):
            z = z_pool.tile([P, D], F32)
            z_out = z[:].rearrange("i (t p) -> i t p", t=PACK)
            x_in = x_sb[:, lane, :].rearrange("i (p t) -> i t p", t=PACK)
            j, e = divmod(lane, PAIR)
            if engine is nc.scalar:
                nc.scalar.activation(
                    out=z_out,
                    in_=x_in,
                    func=ACT.Identity,
                    scale=rstd[j][:, e : e + 1],
                    bias=shift[j][:, e : e + 1],
                )
            elif engine is nc.vector:
                nc.vector.tensor_scalar(
                    out=z_out,
                    in0=x_in,
                    scalar1=mean_var[:, lane, 0:1],
                    scalar2=rstd[j][:, e : e + 1],
                    op0=ALU.subtract,
                    op1=ALU.mult,
                )
            else:
                nc.gpsimd.tensor_scalar(
                    out=z_out,
                    in0=x_in,
                    scalar1=rstd[j][:, e : e + 1],
                    scalar2=shift[j][:, e : e + 1],
                    op0=ALU.mult,
                    op1=ALU.add,
                )
            return z

        def new_z_banks():
            return [
                z_psum.tile([P, 2, PAIR * P], F32, name="z_bank%d" % b, tag="z_bank%d" % b)
                for b in range(2)
            ]

        def transpose(lane, z, z_banks):
            u = lane % ROW_LANES
            permutation = take_below_right if u < 2 else take_below
            e = lane % PAIR
            for t in range(PACK):
                nc.tensor.transpose(
                    out=z_banks[t // 2][:, t % 2, e * P : (e + 1) * P],
                    in_=z[:, t * P : (t + 1) * P],
                    identity=permutation[:],
                )

        h_planes = [stage.tile([P, PACK, PAIR * P], BF16, name="h_planes%d" % j) for j in range(4)]
        h_grouped = [
            stage.tile([P, PAIR * P, PACK], BF16, align_bytes=64, name="h_grouped%d" % j)
            for j in range(4)
        ]

        def gain_out_of_psum(j, z_banks, t, engine):
            z_bank = z_banks[t // 2][:, t % 2, :]
            gain = gain_cols[:, t : t + 1]
            bias = gain_cols[:, PACK + t : PACK + t + 1]
            if engine is nc.scalar:
                nc.scalar.activation(
                    out=h_planes[j][:, t, :], in_=z_bank, func=ACT.Identity, scale=gain, bias=bias
                )
            else:
                nc.vector.tensor_scalar(
                    out=h_planes[j][:, t, :],
                    in0=z_bank,
                    scalar1=gain,
                    scalar2=bias,
                    op0=ALU.mult,
                    op1=ALU.add,
                )

        def pair_cols(j):
            q0 = (PAIR * j + 2) % ROW_LANES
            return j // 2, slice(q0 * P, (q0 + PAIR) * P)

        def quantise_h(j):
            r, rows = pair_cols(j)
            quantise(h_grouped[j][:], s_codes[:, r, rows], s_scales[:, r, rows])

        w_grouped = [
            stage.tile([P, D, PACK], BF16, align_bytes=64, name="w_grouped%d" % s)
            for s in range(PARTS)
        ]
        lo = slice(0, PASS_COLS)
        hi = slice(PASS_COLS, D)
        full = slice(0, D)

        def regroup_w(engine, s, cols, pieces=1):
            width = (cols.stop - cols.start) // pieces
            for c0 in range(cols.start, cols.stop, width):
                part = slice(c0, c0 + width)
                regroup(engine, w_sb[:, s, :, part], w_grouped[s][:, part, :])

        def quantise_w(s, cols):
            quantise(w_grouped[s][:, cols, :], w_codes[:, s, cols], w_scales[:, s, cols])

        def group_out(s, n0, heads, lane0):
            return out_sb[
                :, s, n0 : n0 + heads, lane0 : lane0 + BANK_LANES, :
            ].rearrange("m n q c -> m q n c")

        def bias_of(s, n0, heads):
            return (
                bias_all[:, s, n0 * HEAD_DIM : (n0 + heads) * HEAD_DIM]
                .rearrange("m (o n c) -> m o n c", o=1, c=HEAD_DIM)
                .to_broadcast([P, BANK_LANES, heads, HEAD_DIM])
            )

        def multiply(j, s, n0, heads, pool, tag):
            r, rows0 = pair_cols(j)
            cols = slice(n0 * HEAD_DIM, (n0 + heads) * HEAD_DIM)
            acc = pool.tile([P, BANK_LANES, heads * HEAD_DIM], F32, name="acc", tag=tag)
            for e in range(BANK_LANES):
                rows = slice(rows0.start + e * P, rows0.start + (e + 1) * P)
                nc.tensor.matmul_mx(
                    out=acc[:, e, :],
                    lhsT=s_codes[:, r, rows].bitcast(FP8X4),
                    lhsT_scale=s_scales[:, r, rows],
                    rhs=w_codes[:, s, cols].bitcast(FP8X4),
                    rhs_scale=w_scales[:, s, cols],
                    start=True,
                    stop=True,
                )
            return acc

        def out_of_bank(j, s, n0, heads):
            r, rows0 = pair_cols(j)
            return group_out(s, n0, heads, r * ROW_LANES + rows0.start // P)

        def vec(j, s, n0, heads=PASS_HEADS):
            acc = multiply(j, s, n0, heads, acc_psum, "acc")
            nc.vector.tensor_tensor(
                out=out_of_bank(j, s, n0, heads),
                in0=acc[:].rearrange("m q (n c) -> m q n c", c=HEAD_DIM),
                in1=bias_of(s, n0, heads),
                op=ALU.add,
            )

        def store(r, s, n0, heads=PASS_HEADS):
            dram = outs[s].rearrange("w n (h r q) c -> h r w n (q c)", h=2, r=ROUNDS)
            for half in range(2):
                nc.sync.dma_start(
                    out=dram[half, r, :, n0 : n0 + heads, :],
                    in_=out_sb[
                        half:P:2,
                        s,
                        n0 : n0 + heads,
                        r * ROW_LANES : (r + 1) * ROW_LANES,
                        :,
                    ].rearrange("m n q c -> m n (q c)"),
                )

        def store_both(s, n0, heads):
            dram = outs[s].rearrange("w n (h p) c -> h w n (p c)", h=2)
            for half in range(2):
                nc.sync.dma_start(
                    out=dram[half, :, n0 : n0 + heads, :],
                    in_=out_sb[half:P:2, s, n0 : n0 + heads, :, :].rearrange("m n p c -> m n (p c)"),
                )

        H = PASS_HEADS
        V, S, G = nc.vector, nc.scalar, nc.gpsimd
        nc.gpsimd.tensor_copy(out=gain_cols[:, 0:PACK], in_=gain_raw[:])
        nc.gpsimd.tensor_copy(out=gain_cols[:, PACK : 2 * PACK], in_=bias_raw[:])
        row_stats(0)
        row_stats(1)
        mean_on_scalar(3)
        row_moments(0)
        row_std(0)
        dev_sum_on_scalar(3)
        row_stats(2)
        pair_rstd(0)
        lane_moments(2)
        lane_std(2, False)
        lane_std(3, True)
        z1 = normalise(1, V)
        z0 = normalise(0, V)
        zA = new_z_banks()
        transpose(1, z1, zA)
        transpose(0, z0, zA)
        regroup_w(S, 0, lo)
        pair_rstd(1)
        z2 = normalise(2, V)
        z3 = normalise(3, V)
        for t in range(4):
            gain_out_of_psum(0, zA, t, S)
        row_stats(4)
        row_stats(5)
        row_moments(2)
        zB = new_z_banks()
        transpose(2, z2, zB)
        transpose(3, z3, zB)
        idle_passes(2)
        for t in range(4):
            gain_out_of_psum(1, zB, t, S)
        regroup(V, h_planes[0][:], h_grouped[0][:])
        quantise_w(0, lo)
        quantise_h(0)
        row_std(2)
        regroup_w(S, 0, hi)
        regroup(V, h_planes[1][:], h_grouped[1][:])
        regroup_w(S, 1, lo)
        pair_rstd(2)
        quantise_h(1)
        quantise_w(0, hi)
        pair_shift(2)
        z4 = normalise(4, G)
        z5 = normalise(5, G)
        vec(0, 0, 0)
        mean_on_scalar(7)
        regroup_w(S, 1, hi)
        dev_sum_on_scalar(7)
        vec(1, 0, 0)
        store(0, 0, 0)
        row_stats(6)
        vec(0, 0, H)
        lane_moments(6)
        quantise_w(1, lo)
        vec(1, 0, H)
        store(0, 0, H)
        lane_std(6, False)
        lane_std(7, True)
        pair_rstd(3)
        quantise_w(1, hi)
        pair_shift(3)
        z6 = normalise(6, G)
        z7 = normalise(7, G)
        zC = new_z_banks()
        transpose(4, z4, zC)
        transpose(5, z5, zC)
        regroup_w(S, 2, lo)
        for t in range(4):
            gain_out_of_psum(2, zC, t, S)
        vec(0, 1, 0)
        vec(1, 1, 0)
        store(0, 1, 0)
        vec(0, 1, H)
        quantise_w(2, lo)
        regroup_w(S, 2, hi)
        vec(1, 1, H)
        store(0, 1, H)
        regroup(S, h_planes[2][:], h_grouped[2][:])
        vec(0, 2, 0)
        zD = new_z_banks()
        transpose(6, z6, zD)
        transpose(7, z7, zD)
        for t in range(4):
            gain_out_of_psum(3, zD, t, S)
        regroup(S, h_planes[3][:], h_grouped[3][:])
        quantise_w(2, hi)
        vec(1, 2, 0)
        store(0, 2, 0)
        quantise_h(2)
        vec(0, 2, H)
        vec(1, 2, H)
        store(0, 2, H)
        vec(2, 0, 0)
        quantise_h(3)
        vec(2, 0, H)
        vec(3, 0, 0)
        store(1, 0, 0)
        vec(3, 0, H)
        store(1, 0, H)
        for n0 in (0, H):
            vec(2, 1, n0)
            vec(3, 1, n0)
            store(1, 1, n0)
        vec(2, 2, 0)
        vec(3, 2, 0)
        store(1, 2, 0)
        for n0 in (H, H + 2):
            vec(2, 2, n0, 2)
            vec(3, 2, n0, 2)
            store(1, 2, n0, 2)
